import numpy as np
import ml_dtypes


def mxq(x, axis, fmt="e4m3"):
    dtype, down = {"e4m3": (ml_dtypes.float8_e4m3fn, 7), "e5m2": (ml_dtypes.float8_e5m2, 14)}[fmt]
    v = np.moveaxis(np.asarray(x, np.float32).astype(ml_dtypes.bfloat16).astype(np.float64), axis, -1)
    blocks = v.reshape(v.shape[:-1] + (-1, 32))
    amax = np.abs(blocks).max(-1, keepdims=True)
    byte = np.maximum(np.where(amax > 0, np.frexp(amax)[1] - 1 + 127, 0) - down, 1)
    scale = np.exp2(byte - 127.0)
    codes = (blocks / scale).astype(np.float32).astype(dtype).astype(np.float64)
    return np.moveaxis((codes * scale).reshape(v.shape), -1, axis)


WIDE = False


def mx_kscale(k):
    if not WIDE:
        return np.ones(k)
    levels = np.array([10, -10, 5, -5, 0])
    a = np.random.permutation(np.resize(levels, k // 512 * 4)).reshape(k // 512, 4)
    idx = np.arange(k)
    return np.exp2(a[idx // 512, idx % 128 // 32])


BF16 = ml_dtypes.bfloat16


def bf(x):
    return np.asarray(x, np.float32).astype(BF16)


def f64(x):
    return np.asarray(x).astype(np.float64)


B, D, S, N = 1024, 2048, 4, 128
DS = D // S


def sigmoid(v):
    return 1.0 / (1.0 + np.exp(-v))


def setup_inputs():
    s = mx_kscale(D)
    t = np.maximum(1.0 + 2.0 * np.random.standard_normal((B, N, S)), 0.0) + np.maximum(1.0 + 2.0 * np.random.standard_normal((B, N, S)), 0.0)
    return {"a": bf(t * t / (t * t).sum(axis=1, keepdims=True)),
            "vr": bf(np.random.standard_normal((N, S, DS)) * 0.5 * np.sqrt(N) * s.reshape(S, DS)),
            "h": bf(np.random.standard_normal((B, D)) * s),
            "x2g": bf(np.random.standard_normal((B, D))),
            "w_g": bf(np.random.standard_normal((D, D)) / np.sqrt(D) / s),
            "b_g": bf(np.random.standard_normal(D) * 0.3),
            "bg": bf(1.0 + 0.1 * np.random.standard_normal(1))}


def reference(a, vr, h, x2g, w_g, b_g, bg):
    hf = f64(h)
    hh = (f64(a).transpose(2, 0, 1) @ f64(vr).transpose(1, 0, 2)).transpose(1, 0, 2).reshape(B, D)
    h2g = (mxq(hf, 1, "e4m3") @ mxq(f64(w_g), 1, "e4m3").T) + f64(b_g)
    g = sigmoid(f64(x2g) + h2g + f64(bg))
    return g * hh + (1.0 - g) * hf

@@ -1,0 +1,307 @@
+from contextlib import ExitStack
+
+import concourse.mybir as mybir
+from concourse.masks import make_identity
+
+F32 = mybir.dt.float32
+BF16 = mybir.dt.bfloat16
+U32 = mybir.dt.uint32
+U8 = mybir.dt.uint8
+FP8X4 = mybir.dt.float8_e4m3fn_x4
+ADD = mybir.AluOpType.add
+SUBTRACT = mybir.AluOpType.subtract
+MULT = mybir.AluOpType.mult
+SIGMOID = mybir.ActivationFunctionType.Sigmoid
+
+P = 128
+BATCH = 1024
+FEATURES = 2048
+ROLES = 128
+SLICES = 4
+SLICE = FEATURES // SLICES
+BATCH_TILES = BATCH // P
+W_TILES = SLICE // P
+PACK = 4
+PASSES = FEATURES // (P * PACK)
+STEPS = SLICES * BATCH_TILES
+FIRST_W_ROUND = 3
+
+FLOPS = 2 * BATCH * FEATURES * FEATURES + 2 * BATCH * ROLES * FEATURES
+
+
+def subtract_on_tensor_engine(i):
+    return i % 4 != 3
+
+
+def tile_tpru_pb_kernel(tc, a, vr, h, x2g, w_g, b_g, bg, out):
+    nc = tc.nc
+    with ExitStack() as ctx:
+        const = ctx.enter_context(tc.tile_pool(name="const", bufs=1))
+        h_pool = ctx.enter_context(tc.tile_pool(name="h", bufs=BATCH_TILES))
+        h_mx_pool = ctx.enter_context(tc.tile_pool(name="h_mx", bufs=BATCH_TILES))
+        a_pool = ctx.enter_context(tc.tile_pool(name="a", bufs=BATCH_TILES // 2))
+        w_pool = ctx.enter_context(tc.tile_pool(name="w", bufs=2 * W_TILES))
+        w_mx_pool = ctx.enter_context(tc.tile_pool(name="w_mx", bufs=2))
+        slice_pool = ctx.enter_context(tc.tile_pool(name="slice", bufs=2))
+        x_pool = ctx.enter_context(tc.tile_pool(name="x", bufs=BATCH_TILES + 2))
+        stage = ctx.enter_context(tc.tile_pool(name="stage", bufs=4))
+        work = ctx.enter_context(tc.tile_pool(name="work", bufs=4))
+        psum_t = ctx.enter_context(tc.psum_pool(name="psum_t", bufs=3))
+        psum_z = ctx.enter_context(tc.psum_pool(name="psum_z", bufs=2))
+        psum_d = ctx.enter_context(tc.psum_pool(name="psum_d", bufs=3))
+
+        ident = const.tile([P, P], F32)
+        make_identity(nc, ident[:])
+        ident_bf = const.tile([P, P], BF16)
+        make_identity(nc, ident_bf[:])
+        minus_ident = const.tile([P, P], BF16)
+        nc.vector.tensor_scalar_mul(out=minus_ident[:], in0=ident_bf[:], scalar1=-1.0)
+        bg_col = const.tile([P, 1], BF16)
+
+        h_rows = {}
+        h_codes = {}
+        h_scales = {}
+        a_rows = {}
+        roles = {}
+        w_rows = {}
+        w_codes = {}
+        w_scales = {}
+        vr_slice = {}
+        bias_slice = {}
+        x_rows = {}
+        x_biased = {}
+        h_regrouped = {}
+        w_regrouped = {}
+        z_bank = {}
+        d_bank = {}
+        gate = {}
+        product = {}
+        result = {}
+
+        def load_w(s, c):
+            rows = w_pool.tile([P, FEATURES], BF16)
+            first = s * SLICE + c * P
+            nc.sync.dma_start(out=rows[:], in_=w_g[first : first + P, :])
+            w_rows[(s, c)] = rows
+
+        def load_h(i):
+            rows = h_pool.tile([P, FEATURES], BF16)
+            nc.sync.dma_start(out=rows[:], in_=h[i * P : (i + 1) * P, :])
+            h_rows[i] = rows
+
+        def load_a(pair):
+            rows = a_pool.tile([P, 2 * ROLES * SLICES], BF16)
+            nc.sync.dma_start(
+                out=rows[:].rearrange("p (j f) -> p j f", j=2),
+                in_=a[2 * pair * P : (2 * pair + 2) * P].rearrange("(j p) n s -> p j (n s)", p=P),
+            )
+            a_rows[pair] = rows
+
+        def load_slice_constants(s):
+            vr_s = slice_pool.tile([P, SLICE], BF16)
+            nc.sync.dma_start(out=vr_s[:], in_=vr[:, s, :])
+            vr_slice[s] = vr_s
+            bias_s = slice_pool.tile([P, SLICE], BF16)
+            nc.sync.dma_start(
+                out=bias_s[:], in_=b_g[s * SLICE : (s + 1) * SLICE].partition_broadcast(P)
+            )
+            bias_slice[s] = bias_s
+
+        def load_x(step):
+            s, i = divmod(step, BATCH_TILES)
+            rows = x_pool.tile([P, SLICE], BF16)
+            nc.sync.dma_start(
+                out=rows[:], in_=x2g[i * P : (i + 1) * P, s * SLICE : (s + 1) * SLICE]
+            )
+            x_rows[step] = rows
+
+        def transpose_and_regroup(rows):
+            words = rows[:].bitcast(F32)
+            regrouped = stage.tile([P, FEATURES], BF16, align_bytes=64)
+            regrouped_words = regrouped[:].bitcast(F32).rearrange(
+                "p (g r u) -> p g r u", g=PASSES, u=2
+            )
+            for half in range(2):
+                bank = psum_t.tile([P, 4 * P], F32, tag="bank")
+                for q in range(4):
+                    first = (4 * half + q) * P
+                    nc.tensor.transpose(
+                        bank[:, q * P : (q + 1) * P], words[:, first : first + P], ident[:]
+                    )
+                nc.scalar.copy(
+                    out=regrouped_words[:, 2 * half : 2 * half + 2],
+                    in_=bank[:].rearrange("p (g u r) -> p g r u", g=2, u=2),
+                )
+            return regrouped
+
+        def quantise_h(i, regrouped):
+            codes = h_mx_pool.tile([P, PASSES * P], U32, align_bytes=64)
+            scales = h_mx_pool.tile([P, PASSES * P], U8, align_bytes=64)
+            nc.vector.quantize_mx(out=codes[:].bitcast(FP8X4), scales=scales[:], in_=regrouped[:])
+            h_codes[i] = codes
+            h_scales[i] = scales
+
+        def quantise_w(s, c, regrouped):
+            if c == 0:
+                codes = w_mx_pool.tile([P, PASSES * SLICE], U32, align_bytes=64)
+                scales = w_mx_pool.tile([P, PASSES * SLICE], U8, align_bytes=64)
+                w_codes[s] = codes
+                w_scales[s] = scales
+            for g in range(PASSES):
+                first = g * SLICE + c * P
+                nc.vector.quantize_mx(
+                    out=w_codes[s][:, first : first + P].bitcast(FP8X4),
+                    scales=w_scales[s][:, first : first + P],
+                    in_=regrouped[:, g * P * PACK : (g + 1) * P * PACK],
+                )
+
+        def transpose_roles(pair):
+            words = a_rows[pair][:].bitcast(F32).rearrange("p (j n w) -> p j w n", j=2, w=2)
+            bank = psum_t.tile([P, 4 * P], F32, tag="bank")
+            for j in range(2):
+                for w in range(2):
+                    c = 2 * j + w
+                    nc.tensor.transpose(bank[:, c * P : (c + 1) * P], words[:, j, w, :], ident[:])
+            by_slice = a_pool.tile([P, 2 * SLICES * P], BF16)
+            nc.scalar.copy(
+                out=by_slice[:].rearrange("p (c e b) -> p c e b", c=4, e=2),
+                in_=bank[:].bitcast(BF16).rearrange("p (c b e) -> p c e b", c=4, e=2),
+            )
+            roles[pair] = by_slice
+
+        def add_bias(step):
+            s = step // BATCH_TILES
+            biased = work.tile([P, SLICE], F32)
+            nc.gpsimd.tensor_tensor(
+                out=biased[:], in0=x_rows[step][:], in1=bias_slice[s][:], op=ADD
+            )
+            x_biased[step] = biased
+
+        def multiply(step):
+            s, i = divmod(step, BATCH_TILES)
+            z = psum_z.tile([P, SLICE], F32)
+            for g in range(PASSES):
+                nc.tensor.matmul_mx(
+                    out=z[:],
+                    lhsT=h_codes[i][:, g * P : (g + 1) * P].bitcast(FP8X4),
+                    lhsT_scale=h_scales[i][:, g * P : (g + 1) * P],
+                    rhs=w_codes[s][:, g * SLICE : (g + 1) * SLICE].bitcast(FP8X4),
+                    rhs_scale=w_scales[s][:, g * SLICE : (g + 1) * SLICE],
+                    start=(g == 0),
+                    stop=(g == PASSES - 1),
+                )
+            z_bank[step] = z
+            d = psum_d.tile([P, SLICE], F32)
+            first = ((i % 2) * SLICES + s) * P
+            nc.tensor.matmul(
+                out=d[:],
+                lhsT=roles[i // 2][:, first : first + P],
+                rhs=vr_slice[s][:],
+                start=True,
+                stop=not subtract_on_tensor_engine(i),
+            )
+            if subtract_on_tensor_engine(i):
+                nc.tensor.matmul(
+                    out=d[:],
+                    lhsT=minus_ident[:],
+                    rhs=h_rows[i][:, s * SLICE : (s + 1) * SLICE],
+                    start=False,
+                    stop=True,
+                )
+            d_bank[step] = d
+
+        def open_gate(step):
+            logits = work.tile([P, SLICE], F32)
+            nc.vector.tensor_tensor(
+                out=logits[:], in0=z_bank[step][:], in1=x_biased[step][:], op=ADD
+            )
+            g_tile = work.tile([P, SLICE], F32)
+            nc.scalar.activation(
+                out=g_tile[:], in_=logits[:], func=SIGMOID, bias=bg_col[:, 0:1], scale=1.0
+            )
+            gate[step] = g_tile
+
+        def weigh(step):
+            s, i = divmod(step, BATCH_TILES)
+            difference = d_bank[step]
+            if not subtract_on_tensor_engine(i):
+                difference = work.tile([P, SLICE], F32)
+                nc.vector.tensor_tensor(
+                    out=difference[:],
+                    in0=d_bank[step][:],
+                    in1=h_rows[i][:, s * SLICE : (s + 1) * SLICE],
+                    op=SUBTRACT,
+                )
+            weighed = work.tile([P, SLICE], F32)
+            nc.vector.tensor_tensor(out=weighed[:], in0=difference[:], in1=gate[step][:], op=MULT)
+            product[step] = weighed
+
+        def blend(step):
+            s, i = divmod(step, BATCH_TILES)
+            blended = work.tile([P, SLICE], F32)
+            nc.vector.tensor_tensor(
+                out=blended[:],
+                in0=product[step][:],
+                in1=h_rows[i][:, s * SLICE : (s + 1) * SLICE],
+                op=ADD,
+            )
+            result[step] = blended
+
+        def store(step):
+            s, i = divmod(step, BATCH_TILES)
+            nc.sync.dma_start(
+                out=out[i * P : (i + 1) * P, s * SLICE : (s + 1) * SLICE], in_=result[step][:]
+            )
+
+        for c in range(W_TILES):
+            load_w(0, c)
+        for i in range(BATCH_TILES):
+            load_h(i)
+            if i == 0:
+                load_slice_constants(0)
+                nc.sync.dma_start(out=bg_col[:], in_=bg.partition_broadcast(P))
+            if i % 2 == 0:
+                load_a(i // 2)
+            load_x(i)
+            if i >= BATCH_TILES - W_TILES:
+                load_w(1, i - (BATCH_TILES - W_TILES))
+
+        for c in range(W_TILES):
+            quantise_w(0, c, transpose_and_regroup(w_rows[(0, c)]))
+        for i in range(2):
+            quantise_h(i, transpose_and_regroup(h_rows[i]))
+        transpose_roles(0)
+        add_bias(0)
+        add_bias(1)
+
+        for n in range(STEPS + 4):
+            s, i = divmod(n, BATCH_TILES)
+            if n >= 4:
+                store(n - 4)
+            if n < STEPS - BATCH_TILES:
+                load_x(n + BATCH_TILES)
+                if i == 0:
+                    load_slice_constants(s + 1)
+                if i < W_TILES and s + 2 < SLICES:
+                    load_w(s + 2, i)
+            if n + 2 < STEPS:
+                add_bias(n + 2)
+            for i_next, regrouped in h_regrouped.get(n - 1, []):
+                quantise_h(i_next, regrouped)
+            for s_next, c, regrouped in w_regrouped.get(n - 1, []):
+                quantise_w(s_next, c, regrouped)
+            if n < STEPS:
+                multiply(n)
+            if 0 <= n - 1 < STEPS:
+                open_gate(n - 1)
+            if 0 <= n - 2 < STEPS:
+                weigh(n - 2)
+            if 0 <= n - 3 < STEPS:
+                blend(n - 3)
+            if s == 0 and i + 2 < BATCH_TILES:
+                h_regrouped[n] = [(i + 2, transpose_and_regroup(h_rows[i + 2]))]
+                if i % 2 == 0:
+                    transpose_roles((i + 2) // 2)
+            if s + 1 < SLICES and FIRST_W_ROUND <= i < FIRST_W_ROUND + W_TILES:
+                c = i - FIRST_W_ROUND
+                w_regrouped[n] = [(s + 1, c, transpose_and_regroup(w_rows[(s + 1, c)]))]

@@ -49,6 +49,7 @@ def tile_tpru_pb_kernel(tc, a, vr, h, x2g, w_g, b_g, bg, out):
         psum_t = ctx.enter_context(tc.psum_pool(name="psum_t", bufs=3))
         psum_z = ctx.enter_context(tc.psum_pool(name="psum_z", bufs=2))
         psum_d = ctx.enter_context(tc.psum_pool(name="psum_d", bufs=3))
+        ctx.enter_context(tc.manual_schedule())
 
         ident = const.tile([P, P], F32)
         make_identity(nc, ident[:])
@@ -70,8 +71,6 @@ def tile_tpru_pb_kernel(tc, a, vr, h, x2g, w_g, b_g, bg, out):
         bias_slice = {}
         x_rows = {}
         x_biased = {}
-        h_regrouped = {}
-        w_regrouped = {}
         z_bank = {}
         d_bank = {}
         gate = {}
@@ -276,6 +275,8 @@ def tile_tpru_pb_kernel(tc, a, vr, h, x2g, w_g, b_g, bg, out):
 
         for n in range(STEPS + 4):
             s, i = divmod(n, BATCH_TILES)
+            h_is_due = s == 0 and i + 2 < BATCH_TILES
+            w_is_due = s + 1 < SLICES and FIRST_W_ROUND <= i < FIRST_W_ROUND + W_TILES
             if n >= 4:
                 store(n - 4)
             if n < STEPS - BATCH_TILES:
@@ -286,10 +287,12 @@ def tile_tpru_pb_kernel(tc, a, vr, h, x2g, w_g, b_g, bg, out):
                     load_w(s + 2, i)
             if n + 2 < STEPS:
                 add_bias(n + 2)
-            for i_next, regrouped in h_regrouped.get(n - 1, []):
-                quantise_h(i_next, regrouped)
-            for s_next, c, regrouped in w_regrouped.get(n - 1, []):
-                quantise_w(s_next, c, regrouped)
+            if h_is_due:
+                h_regrouped = transpose_and_regroup(h_rows[i + 2])
+                if i % 2 == 0:
+                    transpose_roles((i + 2) // 2)
+            if w_is_due:
+                w_regrouped = transpose_and_regroup(w_rows[(s + 1, i - FIRST_W_ROUND)])
             if n < STEPS:
                 multiply(n)
             if 0 <= n - 1 < STEPS:
@@ -298,10 +301,7 @@ def tile_tpru_pb_kernel(tc, a, vr, h, x2g, w_g, b_g, bg, out):
                 weigh(n - 2)
             if 0 <= n - 3 < STEPS:
                 blend(n - 3)
-            if s == 0 and i + 2 < BATCH_TILES:
-                h_regrouped[n] = [(i + 2, transpose_and_regroup(h_rows[i + 2]))]
-                if i % 2 == 0:
-                    transpose_roles((i + 2) // 2)
-            if s + 1 < SLICES and FIRST_W_ROUND <= i < FIRST_W_ROUND + W_TILES:
-                c = i - FIRST_W_ROUND
-                w_regrouped[n] = [(s + 1, c, transpose_and_regroup(w_rows[(s + 1, c)]))]
+            if h_is_due:
+                quantise_h(i + 2, h_regrouped)
+            if w_is_due:
+                quantise_w(s + 1, i - FIRST_W_ROUND, w_regrouped)

@@ -29,8 +29,8 @@ FIRST_W_ROUND = 3
 FLOPS = 2 * BATCH * FEATURES * FEATURES + 2 * BATCH * ROLES * FEATURES
 
 
-def subtract_on_tensor_engine(i):
-    return i % 4 != 3
+def subtract_on_tensor_engine(step):
+    return step % 3 != 2
 
 
 def tile_tpru_pb_kernel(tc, a, vr, h, x2g, w_g, b_g, bg, out):
@@ -48,7 +48,8 @@ def tile_tpru_pb_kernel(tc, a, vr, h, x2g, w_g, b_g, bg, out):
         work = ctx.enter_context(tc.tile_pool(name="work", bufs=4))
         psum_t = ctx.enter_context(tc.psum_pool(name="psum_t", bufs=3))
         psum_z = ctx.enter_context(tc.psum_pool(name="psum_z", bufs=2))
-        psum_d = ctx.enter_context(tc.psum_pool(name="psum_d", bufs=3))
+        psum_d = ctx.enter_context(tc.psum_pool(name="psum_d", bufs=2))
+        psum_b = ctx.enter_context(tc.psum_pool(name="psum_b", bufs=1))
         ctx.enter_context(tc.manual_schedule())
 
         ident = const.tile([P, P], F32)
@@ -58,6 +59,10 @@ def tile_tpru_pb_kernel(tc, a, vr, h, x2g, w_g, b_g, bg, out):
         minus_ident = const.tile([P, P], BF16)
         nc.vector.tensor_scalar_mul(out=minus_ident[:], in0=ident_bf[:], scalar1=-1.0)
         bg_col = const.tile([P, 1], BF16)
+        ones = const.tile([P, P], BF16)
+        nc.vector.memset(ones[:], 1.0)
+        bias_rows = const.tile([P, FEATURES], BF16)
+        nc.vector.memset(bias_rows[:], 0.0)
 
         h_rows = {}
         h_codes = {}
@@ -68,9 +73,12 @@ def tile_tpru_pb_kernel(tc, a, vr, h, x2g, w_g, b_g, bg, out):
         w_codes = {}
         w_scales = {}
         vr_slice = {}
-        bias_slice = {}
+        bias_bank = {}
+        difference = {}
         x_rows = {}
         x_biased = {}
+        h_regrouped = {}
+        w_regrouped = {}
         z_bank = {}
         d_bank = {}
         gate = {}
@@ -96,15 +104,10 @@ def tile_tpru_pb_kernel(tc, a, vr, h, x2g, w_g, b_g, bg, out):
             )
             a_rows[pair] = rows
 
-        def load_slice_constants(s):
+        def load_vr(s):
             vr_s = slice_pool.tile([P, SLICE], BF16)
             nc.sync.dma_start(out=vr_s[:], in_=vr[:, s, :])
             vr_slice[s] = vr_s
-            bias_s = slice_pool.tile([P, SLICE], BF16)
-            nc.sync.dma_start(
-                out=bias_s[:], in_=b_g[s * SLICE : (s + 1) * SLICE].partition_broadcast(P)
-            )
-            bias_slice[s] = bias_s
 
         def load_x(step):
             s, i = divmod(step, BATCH_TILES)
@@ -168,11 +171,22 @@ def tile_tpru_pb_kernel(tc, a, vr, h, x2g, w_g, b_g, bg, out):
             )
             roles[pair] = by_slice
 
+        def spread_bias(s):
+            bank = psum_b.tile([P, SLICE], F32)
+            nc.tensor.matmul(
+                out=bank[:],
+                lhsT=ones[:],
+                rhs=bias_rows[:, s * SLICE : (s + 1) * SLICE],
+                start=True,
+                stop=True,
+            )
+            bias_bank[s] = bank
+
         def add_bias(step):
             s = step // BATCH_TILES
             biased = work.tile([P, SLICE], F32)
-            nc.gpsimd.tensor_tensor(
-                out=biased[:], in0=x_rows[step][:], in1=bias_slice[s][:], op=ADD
+            nc.vector.tensor_tensor(
+                out=biased[:], in0=bias_bank[s][:], in1=x_rows[step][:], op=ADD
             )
             x_biased[step] = biased
 
@@ -197,9 +211,9 @@ def tile_tpru_pb_kernel(tc, a, vr, h, x2g, w_g, b_g, bg, out):
                 lhsT=roles[i // 2][:, first : first + P],
                 rhs=vr_slice[s][:],
                 start=True,
-                stop=not subtract_on_tensor_engine(i),
+                stop=not subtract_on_tensor_engine(step),
             )
-            if subtract_on_tensor_engine(i):
+            if subtract_on_tensor_engine(step):
                 nc.tensor.matmul(
                     out=d[:],
                     lhsT=minus_ident[:],
@@ -207,6 +221,7 @@ def tile_tpru_pb_kernel(tc, a, vr, h, x2g, w_g, b_g, bg, out):
                     start=False,
                     stop=True,
                 )
+                difference[step] = d
             d_bank[step] = d
 
         def open_gate(step):
@@ -220,25 +235,28 @@ def tile_tpru_pb_kernel(tc, a, vr, h, x2g, w_g, b_g, bg, out):
             )
             gate[step] = g_tile
 
-        def weigh(step):
+        def subtract(step):
             s, i = divmod(step, BATCH_TILES)
-            difference = d_bank[step]
-            if not subtract_on_tensor_engine(i):
-                difference = work.tile([P, SLICE], F32)
-                nc.vector.tensor_tensor(
-                    out=difference[:],
-                    in0=d_bank[step][:],
-                    in1=h_rows[i][:, s * SLICE : (s + 1) * SLICE],
-                    op=SUBTRACT,
-                )
+            subtracted = work.tile([P, SLICE], F32)
+            nc.vector.tensor_tensor(
+                out=subtracted[:],
+                in0=d_bank[step][:],
+                in1=h_rows[i][:, s * SLICE : (s + 1) * SLICE],
+                op=SUBTRACT,
+            )
+            difference[step] = subtracted
+
+        def weigh(step):
             weighed = work.tile([P, SLICE], F32)
-            nc.vector.tensor_tensor(out=weighed[:], in0=difference[:], in1=gate[step][:], op=MULT)
+            nc.vector.tensor_tensor(
+                out=weighed[:], in0=difference[step][:], in1=gate[step][:], op=MULT
+            )
             product[step] = weighed
 
         def blend(step):
             s, i = divmod(step, BATCH_TILES)
             blended = work.tile([P, SLICE], F32)
-            nc.vector.tensor_tensor(
+            nc.gpsimd.tensor_tensor(
                 out=blended[:],
                 in0=product[step][:],
                 in1=h_rows[i][:, s * SLICE : (s + 1) * SLICE],
@@ -257,7 +275,8 @@ def tile_tpru_pb_kernel(tc, a, vr, h, x2g, w_g, b_g, bg, out):
         for i in range(BATCH_TILES):
             load_h(i)
             if i == 0:
-                load_slice_constants(0)
+                load_vr(0)
+                nc.sync.dma_start(out=bias_rows[0:1, :], in_=b_g.rearrange("(o d) -> o d", o=1))
                 nc.sync.dma_start(out=bg_col[:], in_=bg.partition_broadcast(P))
             if i % 2 == 0:
                 load_a(i // 2)
@@ -267,41 +286,43 @@ def tile_tpru_pb_kernel(tc, a, vr, h, x2g, w_g, b_g, bg, out):
 
         for c in range(W_TILES):
             quantise_w(0, c, transpose_and_regroup(w_rows[(0, c)]))
-        for i in range(2):
-            quantise_h(i, transpose_and_regroup(h_rows[i]))
+        quantise_h(0, transpose_and_regroup(h_rows[0]))
         transpose_roles(0)
+        spread_bias(0)
+        quantise_h(1, transpose_and_regroup(h_rows[1]))
         add_bias(0)
-        add_bias(1)
 
-        for n in range(STEPS + 4):
+        for n in range(STEPS + 3):
             s, i = divmod(n, BATCH_TILES)
-            h_is_due = s == 0 and i + 2 < BATCH_TILES
-            w_is_due = s + 1 < SLICES and FIRST_W_ROUND <= i < FIRST_W_ROUND + W_TILES
-            if n >= 4:
-                store(n - 4)
+            if n >= 3:
+                store(n - 3)
             if n < STEPS - BATCH_TILES:
                 load_x(n + BATCH_TILES)
                 if i == 0:
-                    load_slice_constants(s + 1)
+                    load_vr(s + 1)
                 if i < W_TILES and s + 2 < SLICES:
                     load_w(s + 2, i)
-            if n + 2 < STEPS:
-                add_bias(n + 2)
-            if h_is_due:
-                h_regrouped = transpose_and_regroup(h_rows[i + 2])
-                if i % 2 == 0:
-                    transpose_roles((i + 2) // 2)
-            if w_is_due:
-                w_regrouped = transpose_and_regroup(w_rows[(s + 1, i - FIRST_W_ROUND)])
+            if 0 <= n - 2 < STEPS:
+                weigh(n - 2)
+                blend(n - 2)
+            if i == BATCH_TILES - 1 and s + 1 < SLICES:
+                spread_bias(s + 1)
             if n < STEPS:
                 multiply(n)
             if 0 <= n - 1 < STEPS:
                 open_gate(n - 1)
-            if 0 <= n - 2 < STEPS:
-                weigh(n - 2)
-            if 0 <= n - 3 < STEPS:
-                blend(n - 3)
-            if h_is_due:
-                quantise_h(i + 2, h_regrouped)
-            if w_is_due:
-                quantise_w(s + 1, i - FIRST_W_ROUND, w_regrouped)
+                if not subtract_on_tensor_engine(n - 1):
+                    subtract(n - 1)
+            if n + 1 < STEPS:
+                add_bias(n + 1)
+            for i_next, regrouped in h_regrouped.get(n - 1, []):
+                quantise_h(i_next, regrouped)
+            for s_next, c, regrouped in w_regrouped.get(n - 1, []):
+                quantise_w(s_next, c, regrouped)
+            if s == 0 and i + 2 < BATCH_TILES:
+                h_regrouped[n] = [(i + 2, transpose_and_regroup(h_rows[i + 2]))]
+                if i % 2 == 0:
+                    transpose_roles((i + 2) // 2)
+            if s + 1 < SLICES and FIRST_W_ROUND <= i < FIRST_W_ROUND + W_TILES:
+                c = i - FIRST_W_ROUND
+                w_regrouped[n] = [(s + 1, c, transpose_and_regroup(w_rows[(s + 1, c)]))]

@@ -46,6 +46,7 @@ def tile_tpru_pb_kernel(tc, a, vr, h, x2g, w_g, b_g, bg, out):
         x_pool = ctx.enter_context(tc.tile_pool(name="x", bufs=BATCH_TILES + 2))
         stage = ctx.enter_context(tc.tile_pool(name="stage", bufs=4))
         work = ctx.enter_context(tc.tile_pool(name="work", bufs=4))
+        out_pool = ctx.enter_context(tc.tile_pool(name="out", bufs=8))
         psum_t = ctx.enter_context(tc.psum_pool(name="psum_t", bufs=3))
         psum_z = ctx.enter_context(tc.psum_pool(name="psum_z", bufs=2))
         psum_d = ctx.enter_context(tc.psum_pool(name="psum_d", bufs=2))
@@ -190,7 +191,7 @@ def tile_tpru_pb_kernel(tc, a, vr, h, x2g, w_g, b_g, bg, out):
             )
             x_biased[step] = biased
 
-        def multiply(step):
+        def multiply_state(step):
             s, i = divmod(step, BATCH_TILES)
             z = psum_z.tile([P, SLICE], F32)
             for g in range(PASSES):
@@ -204,6 +205,9 @@ def tile_tpru_pb_kernel(tc, a, vr, h, x2g, w_g, b_g, bg, out):
                     stop=(g == PASSES - 1),
                 )
             z_bank[step] = z
+
+        def multiply_roles(step):
+            s, i = divmod(step, BATCH_TILES)
             d = psum_d.tile([P, SLICE], F32)
             first = ((i % 2) * SLICES + s) * P
             nc.tensor.matmul(
@@ -255,7 +259,7 @@ def tile_tpru_pb_kernel(tc, a, vr, h, x2g, w_g, b_g, bg, out):
 
         def blend(step):
             s, i = divmod(step, BATCH_TILES)
-            blended = work.tile([P, SLICE], F32)
+            blended = out_pool.tile([P, SLICE], F32)
             nc.gpsimd.tensor_tensor(
                 out=blended[:],
                 in0=product[step][:],
@@ -300,25 +304,25 @@ def tile_tpru_pb_kernel(tc, a, vr, h, x2g, w_g, b_g, bg, out):
                 load_x(n + BATCH_TILES)
                 if i == 0:
                     load_vr(s + 1)
-                if i < W_TILES and s + 2 < SLICES:
-                    load_w(s + 2, i)
+                if i >= BATCH_TILES - W_TILES and s + 2 < SLICES:
+                    load_w(s + 2, i - (BATCH_TILES - W_TILES))
+            if 0 <= n - 1 < STEPS:
+                open_gate(n - 1)
             if 0 <= n - 2 < STEPS:
                 weigh(n - 2)
                 blend(n - 2)
-            if i == BATCH_TILES - 1 and s + 1 < SLICES:
-                spread_bias(s + 1)
-            if n < STEPS:
-                multiply(n)
-            if 0 <= n - 1 < STEPS:
-                open_gate(n - 1)
-                if not subtract_on_tensor_engine(n - 1):
-                    subtract(n - 1)
-            if n + 1 < STEPS:
-                add_bias(n + 1)
             for i_next, regrouped in h_regrouped.get(n - 1, []):
                 quantise_h(i_next, regrouped)
             for s_next, c, regrouped in w_regrouped.get(n - 1, []):
                 quantise_w(s_next, c, regrouped)
+            if 0 <= n - 1 < STEPS and not subtract_on_tensor_engine(n - 1):
+                subtract(n - 1)
+            if n + 1 < STEPS:
+                if (n + 1) % BATCH_TILES == 0:
+                    spread_bias((n + 1) // BATCH_TILES)
+                add_bias(n + 1)
+            if n < STEPS:
+                multiply_state(n)
             if s == 0 and i + 2 < BATCH_TILES:
                 h_regrouped[n] = [(i + 2, transpose_and_regroup(h_rows[i + 2]))]
                 if i % 2 == 0:
@@ -326,3 +330,5 @@ def tile_tpru_pb_kernel(tc, a, vr, h, x2g, w_g, b_g, bg, out):
             if s + 1 < SLICES and FIRST_W_ROUND <= i < FIRST_W_ROUND + W_TILES:
                 c = i - FIRST_W_ROUND
                 w_regrouped[n] = [(s + 1, c, transpose_and_regroup(w_rows[(s + 1, c)]))]
+            if n < STEPS:
+                multiply_roles(n)

from contextlib import ExitStack

import concourse.mybir as mybir
from concourse.masks import make_identity

F32 = mybir.dt.float32
BF16 = mybir.dt.bfloat16
U32 = mybir.dt.uint32
U8 = mybir.dt.uint8
FP8X4 = mybir.dt.float8_e4m3fn_x4
ADD = mybir.AluOpType.add
SUBTRACT = mybir.AluOpType.subtract
MULT = mybir.AluOpType.mult
SIGMOID = mybir.ActivationFunctionType.Sigmoid

P = 128
BATCH = 1024
FEATURES = 2048
ROLES = 128
SLICES = 4
SLICE = FEATURES // SLICES
BATCH_TILES = BATCH // P
W_TILES = SLICE // P
PACK = 4
PASSES = FEATURES // (P * PACK)
STEPS = SLICES * BATCH_TILES
FIRST_W_ROUND = 3

FLOPS = 2 * BATCH * FEATURES * FEATURES + 2 * BATCH * ROLES * FEATURES


def subtract_on_tensor_engine(step):
    return step % 3 != 2


def tile_tpru_pb_kernel(tc, a, vr, h, x2g, w_g, b_g, bg, out):
    nc = tc.nc
    with ExitStack() as ctx:
        const = ctx.enter_context(tc.tile_pool(name="const", bufs=1))
        h_pool = ctx.enter_context(tc.tile_pool(name="h", bufs=BATCH_TILES))
        h_mx_pool = ctx.enter_context(tc.tile_pool(name="h_mx", bufs=BATCH_TILES))
        a_pool = ctx.enter_context(tc.tile_pool(name="a", bufs=BATCH_TILES // 2))
        w_pool = ctx.enter_context(tc.tile_pool(name="w", bufs=2 * W_TILES))
        w_mx_pool = ctx.enter_context(tc.tile_pool(name="w_mx", bufs=2))
        slice_pool = ctx.enter_context(tc.tile_pool(name="slice", bufs=2))
        x_pool = ctx.enter_context(tc.tile_pool(name="x", bufs=BATCH_TILES + 2))
        stage = ctx.enter_context(tc.tile_pool(name="stage", bufs=4))
        work = ctx.enter_context(tc.tile_pool(name="work", bufs=4))
        out_pool = ctx.enter_context(tc.tile_pool(name="out", bufs=8))
        psum_t = ctx.enter_context(tc.psum_pool(name="psum_t", bufs=3))
        psum_z = ctx.enter_context(tc.psum_pool(name="psum_z", bufs=2))
        psum_d = ctx.enter_context(tc.psum_pool(name="psum_d", bufs=2))
        psum_b = ctx.enter_context(tc.psum_pool(name="psum_b", bufs=1))
        ctx.enter_context(tc.manual_schedule())

        ident = const.tile([P, P], F32)
        make_identity(nc, ident[:])
        ident_bf = const.tile([P, P], BF16)
        make_identity(nc, ident_bf[:])
        minus_ident = const.tile([P, P], BF16)
        nc.vector.tensor_scalar_mul(out=minus_ident[:], in0=ident_bf[:], scalar1=-1.0)
        bg_col = const.tile([P, 1], BF16)
        ones = const.tile([P, P], BF16)
        nc.vector.memset(ones[:], 1.0)
        bias_rows = const.tile([P, FEATURES], BF16)
        nc.vector.memset(bias_rows[:], 0.0)

        h_rows = {}
        h_codes = {}
        h_scales = {}
        a_rows = {}
        roles = {}
        w_rows = {}
        w_codes = {}
        w_scales = {}
        vr_slice = {}
        bias_bank = {}
        difference = {}
        x_rows = {}
        x_biased = {}
        h_regrouped = {}
        w_regrouped = {}
        z_bank = {}
        d_bank = {}
        gate = {}
        product = {}
        result = {}

        def load_w(s, c):
            rows = w_pool.tile([P, FEATURES], BF16)
            first = s * SLICE + c * P
            nc.sync.dma_start(out=rows[:], in_=w_g[first : first + P, :])
            w_rows[(s, c)] = rows

        def load_h(i):
            rows = h_pool.tile([P, FEATURES], BF16)
            nc.sync.dma_start(out=rows[:], in_=h[i * P : (i + 1) * P, :])
            h_rows[i] = rows

        def load_a(pair):
            rows = a_pool.tile([P, 2 * ROLES * SLICES], BF16)
            nc.sync.dma_start(
                out=rows[:].rearrange("p (j f) -> p j f", j=2),
                in_=a[2 * pair * P : (2 * pair + 2) * P].rearrange("(j p) n s -> p j (n s)", p=P),
            )
            a_rows[pair] = rows

        def load_vr(s):
            vr_s = slice_pool.tile([P, SLICE], BF16)
            nc.sync.dma_start(out=vr_s[:], in_=vr[:, s, :])
            vr_slice[s] = vr_s

        def load_x(step):
            s, i = divmod(step, BATCH_TILES)
            rows = x_pool.tile([P, SLICE], BF16)
            nc.sync.dma_start(
                out=rows[:], in_=x2g[i * P : (i + 1) * P, s * SLICE : (s + 1) * SLICE]
            )
            x_rows[step] = rows

        def transpose_and_regroup(rows):
            words = rows[:].bitcast(F32)
            regrouped = stage.tile([P, FEATURES], BF16, align_bytes=64)
            regrouped_words = regrouped[:].bitcast(F32).rearrange(
                "p (g r u) -> p g r u", g=PASSES, u=2
            )
            for half in range(2):
                bank = psum_t.tile([P, 4 * P], F32, tag="bank")
                for q in range(4):
                    first = (4 * half + q) * P
                    nc.tensor.transpose(
                        bank[:, q * P : (q + 1) * P], words[:, first : first + P], ident[:]
                    )
                nc.scalar.copy(
                    out=regrouped_words[:, 2 * half : 2 * half + 2],
                    in_=bank[:].rearrange("p (g u r) -> p g r u", g=2, u=2),
                )
            return regrouped

        def quantise_h(i, regrouped):
            codes = h_mx_pool.tile([P, PASSES * P], U32, align_bytes=64)
            scales = h_mx_pool.tile([P, PASSES * P], U8, align_bytes=64)
            nc.vector.quantize_mx(out=codes[:].bitcast(FP8X4), scales=scales[:], in_=regrouped[:])
            h_codes[i] = codes
            h_scales[i] = scales

        def quantise_w(s, c, regrouped):
            if c == 0:
                codes = w_mx_pool.tile([P, PASSES * SLICE], U32, align_bytes=64)
                scales = w_mx_pool.tile([P, PASSES * SLICE], U8, align_bytes=64)
                w_codes[s] = codes
                w_scales[s] = scales
            for g in range(PASSES):
                first = g * SLICE + c * P
                nc.vector.quantize_mx(
                    out=w_codes[s][:, first : first + P].bitcast(FP8X4),
                    scales=w_scales[s][:, first : first + P],
                    in_=regrouped[:, g * P * PACK : (g + 1) * P * PACK],
                )

        def transpose_roles(pair):
            words = a_rows[pair][:].bitcast(F32).rearrange("p (j n w) -> p j w n", j=2, w=2)
            bank = psum_t.tile([P, 4 * P], F32, tag="bank")
            for j in range(2):
                for w in range(2):
                    c = 2 * j + w
                    nc.tensor.transpose(bank[:, c * P : (c + 1) * P], words[:, j, w, :], ident[:])
            by_slice = a_pool.tile([P, 2 * SLICES * P], BF16)
            nc.scalar.copy(
                out=by_slice[:].rearrange("p (c e b) -> p c e b", c=4, e=2),
                in_=bank[:].bitcast(BF16).rearrange("p (c b e) -> p c e b", c=4, e=2),
            )
            roles[pair] = by_slice

        def spread_bias(s):
            bank = psum_b.tile([P, SLICE], F32)
            nc.tensor.matmul(
                out=bank[:],
                lhsT=ones[:],
                rhs=bias_rows[:, s * SLICE : (s + 1) * SLICE],
                start=True,
                stop=True,
            )
            bias_bank[s] = bank

        def add_bias(step):
            s = step // BATCH_TILES
            biased = work.tile([P, SLICE], F32)
            nc.vector.tensor_tensor(
                out=biased[:], in0=bias_bank[s][:], in1=x_rows[step][:], op=ADD
            )
            x_biased[step] = biased

        def multiply_state(step):
            s, i = divmod(step, BATCH_TILES)
            z = psum_z.tile([P, SLICE], F32)
            for g in range(PASSES):
                nc.tensor.matmul_mx(
                    out=z[:],
                    lhsT=h_codes[i][:, g * P : (g + 1) * P].bitcast(FP8X4),
                    lhsT_scale=h_scales[i][:, g * P : (g + 1) * P],
                    rhs=w_codes[s][:, g * SLICE : (g + 1) * SLICE].bitcast(FP8X4),
                    rhs_scale=w_scales[s][:, g * SLICE : (g + 1) * SLICE],
                    start=(g == 0),
                    stop=(g == PASSES - 1),
                )
            z_bank[step] = z

        def multiply_roles(step):
            s, i = divmod(step, BATCH_TILES)
            d = psum_d.tile([P, SLICE], F32)
            first = ((i % 2) * SLICES + s) * P
            nc.tensor.matmul(
                out=d[:],
                lhsT=roles[i // 2][:, first : first + P],
                rhs=vr_slice[s][:],
                start=True,
                stop=not subtract_on_tensor_engine(step),
            )
            if subtract_on_tensor_engine(step):
                nc.tensor.matmul(
                    out=d[:],
                    lhsT=minus_ident[:],
                    rhs=h_rows[i][:, s * SLICE : (s + 1) * SLICE],
                    start=False,
                    stop=True,
                )
                difference[step] = d
            d_bank[step] = d

        def open_gate(step):
            logits = work.tile([P, SLICE], F32)
            nc.vector.tensor_tensor(
                out=logits[:], in0=z_bank[step][:], in1=x_biased[step][:], op=ADD
            )
            g_tile = work.tile([P, SLICE], F32)
            nc.scalar.activation(
                out=g_tile[:], in_=logits[:], func=SIGMOID, bias=bg_col[:, 0:1], scale=1.0
            )
            gate[step] = g_tile

        def subtract(step):
            s, i = divmod(step, BATCH_TILES)
            subtracted = work.tile([P, SLICE], F32)
            nc.vector.tensor_tensor(
                out=subtracted[:],
                in0=d_bank[step][:],
                in1=h_rows[i][:, s * SLICE : (s + 1) * SLICE],
                op=SUBTRACT,
            )
            difference[step] = subtracted

        def weigh(step):
            weighed = work.tile([P, SLICE], F32)
            nc.vector.tensor_tensor(
                out=weighed[:], in0=difference[step][:], in1=gate[step][:], op=MULT
            )
            product[step] = weighed

        def blend(step):
            s, i = divmod(step, BATCH_TILES)
            blended = out_pool.tile([P, SLICE], F32)
            nc.gpsimd.tensor_tensor(
                out=blended[:],
                in0=product[step][:],
                in1=h_rows[i][:, s * SLICE : (s + 1) * SLICE],
                op=ADD,
            )
            result[step] = blended

        def store(step):
            s, i = divmod(step, BATCH_TILES)
            nc.sync.dma_start(
                out=out[i * P : (i + 1) * P, s * SLICE : (s + 1) * SLICE], in_=result[step][:]
            )

        for c in range(W_TILES):
            load_w(0, c)
        for i in range(BATCH_TILES):
            load_h(i)
            if i == 0:
                load_vr(0)
                nc.sync.dma_start(out=bias_rows[0:1, :], in_=b_g.rearrange("(o d) -> o d", o=1))
                nc.sync.dma_start(out=bg_col[:], in_=bg.partition_broadcast(P))
            if i % 2 == 0:
                load_a(i // 2)
            load_x(i)
            if i >= BATCH_TILES - W_TILES:
                load_w(1, i - (BATCH_TILES - W_TILES))

        for c in range(W_TILES):
            quantise_w(0, c, transpose_and_regroup(w_rows[(0, c)]))
        quantise_h(0, transpose_and_regroup(h_rows[0]))
        transpose_roles(0)
        spread_bias(0)
        quantise_h(1, transpose_and_regroup(h_rows[1]))
        add_bias(0)

        for n in range(STEPS + 3):
            s, i = divmod(n, BATCH_TILES)
            if n >= 3:
                store(n - 3)
            if n < STEPS - BATCH_TILES:
                load_x(n + BATCH_TILES)
                if i == 0:
                    load_vr(s + 1)
                if i >= BATCH_TILES - W_TILES and s + 2 < SLICES:
                    load_w(s + 2, i - (BATCH_TILES - W_TILES))
            if 0 <= n - 1 < STEPS:
                open_gate(n - 1)
            if 0 <= n - 2 < STEPS:
                weigh(n - 2)
                blend(n - 2)
            for i_next, regrouped in h_regrouped.get(n - 1, []):
                quantise_h(i_next, regrouped)
            for s_next, c, regrouped in w_regrouped.get(n - 1, []):
                quantise_w(s_next, c, regrouped)
            if 0 <= n - 1 < STEPS and not subtract_on_tensor_engine(n - 1):
                subtract(n - 1)
            if n + 1 < STEPS:
                if (n + 1) % BATCH_TILES == 0:
                    spread_bias((n + 1) // BATCH_TILES)
                add_bias(n + 1)
            if n < STEPS:
                multiply_state(n)
            if s == 0 and i + 2 < BATCH_TILES:
                h_regrouped[n] = [(i + 2, transpose_and_regroup(h_rows[i + 2]))]
                if i % 2 == 0:
                    transpose_roles((i + 2) // 2)
            if s + 1 < SLICES and FIRST_W_ROUND <= i < FIRST_W_ROUND + W_TILES:
                c = i - FIRST_W_ROUND
                w_regrouped[n] = [(s + 1, c, transpose_and_regroup(w_rows[(s + 1, c)]))]
            if n < STEPS:
                multiply_roles(n)
